import numpy as np
import ml_dtypes


def mxq(x, axis, fmt="e4m3"):
    dtype, down = {"e4m3": (ml_dtypes.float8_e4m3fn, 7), "e5m2": (ml_dtypes.float8_e5m2, 14)}[fmt]
    v = np.moveaxis(np.asarray(x, np.float32).astype(ml_dtypes.bfloat16).astype(np.float64), axis, -1)
    blocks = v.reshape(v.shape[:-1] + (-1, 32))
    amax = np.abs(blocks).max(-1, keepdims=True)
    byte = np.maximum(np.where(amax > 0, np.frexp(amax)[1] - 1 + 127, 0) - down, 1)
    scale = np.exp2(byte - 127.0)
    codes = (blocks / scale).astype(np.float32).astype(dtype).astype(np.float64)
    return np.moveaxis((codes * scale).reshape(v.shape), -1, axis)


WIDE = False


def mx_kscale(k):
    if not WIDE:
        return np.ones(k)
    levels = np.array([10, -10, 5, -5, 0])
    if k % 512:
        return np.exp2(np.random.permutation(np.resize(levels, k // 32))).repeat(32)
    a = np.empty((k // 512, 16))
    for p in range(k // 512):
        a[p, :8] = np.random.permutation(np.resize(levels, 8))
        for g in range(8):
            far = levels[np.abs(levels - a[p, g]) >= 10]
            a[p, g + 8] = far[np.random.randint(len(far))]
    return np.exp2(a.ravel()).repeat(32)


BF16 = ml_dtypes.bfloat16


def bf(x):
    return np.asarray(x, np.float32).astype(BF16)


def f64(x):
    return np.asarray(x).astype(np.float64)


B, T, D, F = 2, 512, 512, 512
BINS = np.array([-1.5, -1.0, -0.5, 0.0, 0.5, 1.0, 1.5])
NB = BINS.shape[0] + 1
INDEX = 0


def setup_inputs():
    s = mx_kscale(D)
    s = s / s[INDEX]
    return {"x": bf(np.random.standard_normal((B, T, D)) * s),
            "W": bf(np.random.standard_normal((NB, D, F)) * 0.5 / np.sqrt(D) / s[None, :, None])}


def reference(x, W):
    x, W = f64(x), f64(W)
    y = x[..., INDEX]
    mem = np.sum(np.where(y[..., None] > BINS, 1.0, 0.0), axis=-1)
    xf = x.reshape(B * T, D)
    memf = mem.reshape(B * T)
    xq = mxq(xf, 1, "e4m3")
    Wq = mxq(W, 1, "e4m3")
    out = np.zeros((B * T, F))
    for k in range(NB):
        sel = np.where(memf == k, 1.0, 0.0)[:, None]
        out = out + sel * (xq @ Wq[k])
    return out.reshape(B, T, F)

@@ -1,0 +1,300 @@
+from contextlib import ExitStack
+
+import concourse.mybir as mybir
+
+FLOPS = 2 * 1024 * 512 * 512 * 8
+
+F32 = mybir.dt.float32
+BF16 = mybir.dt.bfloat16
+U32 = mybir.dt.uint32
+U8 = mybir.dt.uint8
+FP8X4 = mybir.dt.float8_e4m3fn_x4
+ALU = mybir.AluOpType
+ACT = mybir.ActivationFunctionType
+AX = mybir.AxisListType
+
+P = 128
+NT = 8
+D = 512
+F = 512
+NE = 8
+L = 4
+BOUNDS = (-1.5, -1.0, -0.5, 0.0, 0.5, 1.0, 1.5)
+MID = 3
+FV = [352,352,352,352,352,352,352,352]
+X_GROUPS = ((0, 1), (2, 3), (4, 5, 6, 7))
+T_BANKS = ((0, 1), (2, 3), (4, 5), (6, 7), (4, 5), (6, 7), (4, 5), (6, 7))
+W_AFTER = {2: (1,), 4: (2,), 5: (3,)}
+PINNED = True
+
+
+def tile_dispatchbyvariable_pa_kernel(tc, x, W, out):
+    nc = tc.nc
+    x_v = x.flatten_outer_dims().rearrange("(p j) d -> p j d", j=NT)
+    o_v = out.flatten_outer_dims().rearrange("(p j) f -> p j f", j=NT)
+    nb = len(BOUNDS)
+    where = {}
+    for g, tiles in enumerate(X_GROUPS):
+        for i, j in enumerate(tiles):
+            where[j] = (g, i)
+
+    with ExitStack() as ctx:
+        if PINNED:
+            ctx.enter_context(tc.manual_schedule())
+        keep = ctx.enter_context(tc.tile_pool(name="keep", bufs=1))
+        psum = ctx.enter_context(tc.psum_pool(name="psum", bufs=1))
+
+        xh = [keep.tile([P, len(t), D], BF16, name="xh%d" % g) for g, t in enumerate(X_GROUPS)]
+        raw = [keep.tile([P, 4, F], BF16, name="raw%d" % k) for k in range(NE)]
+
+        def load_x(g):
+            t = X_GROUPS[g]
+            nc.sync.dma_start(out=xh[g][:], in_=x_v[:, t[0] : t[0] + len(t), :])
+
+        def load_w(k):
+            nc.sync.dma_start(
+                out=raw[k][:].rearrange("p t f -> p (t f)"),
+                in_=W[k].rearrange("(p t) f -> p (t f)", t=4),
+            )
+
+        load_x(0)
+        load_w(0)
+        load_x(1)
+        load_x(2)
+        for k in range(1, NE):
+            load_w(k)
+
+        col_i = keep.tile([P, L * P], F32, name="col_i")
+        nc.gpsimd.iota(
+            col_i[:], pattern=[[1, L * P]], base=0, channel_multiplier=-1,
+            allow_small_or_imprecise_dtypes=True,
+        )
+        bins = keep.tile([P, nb - 1], F32, name="bins")
+        for i, b in enumerate(BOUNDS[:MID] + BOUNDS[MID + 1 :]):
+            nc.vector.memset(bins[:, i : i + 1], b)
+        warm = keep.tile([P, 1], F32, name="warm")
+        nc.scalar.activation(out=warm[:], in_=bins[:, 0:1], func=ACT.Copy)
+        colv = keep.tile([P, L * P], F32, name="colv")
+        nc.vector.tensor_scalar(
+            out=colv[:], in0=col_i[:], scalar1=1.0 / P, scalar2=float(MID), op0=ALU.mult, op1=ALU.add
+        )
+
+        ncmp = nb - 1 + MID
+        cmp = [keep.tile([P, len(t), ncmp], F32, name="cmp%d" % g) for g, t in enumerate(X_GROUPS)]
+        lo = [keep.tile([P, len(t)], F32, name="lo%d" % g) for g, t in enumerate(X_GROUPS)]
+        hi1 = [keep.tile([P, len(t)], F32, name="hi1_%d" % g) for g, t in enumerate(X_GROUPS)]
+
+        def bucket_cmp(g):
+            n = len(X_GROUPS[g])
+            nc.vector.tensor_tensor(
+                out=cmp[g][:, :, 0 : nb - 1],
+                in0=xh[g][:, :, 0:1].to_broadcast([P, n, nb - 1]),
+                in1=bins[:].unsqueeze(1).to_broadcast([P, n, nb - 1]),
+                op=ALU.is_gt,
+            )
+            nc.vector.tensor_scalar(
+                out=cmp[g][:, :, nb - 1 : ncmp],
+                in0=xh[g][:, :, 0:1].to_broadcast([P, n, MID]),
+                scalar1=BOUNDS[MID], scalar2=0.0, op0=ALU.is_gt, op1=ALU.is_equal,
+            )
+
+        def bucket_sum(g):
+            nc.vector.tensor_reduce(out=lo[g][:], in_=cmp[g][:], axis=AX.X, op=ALU.add)
+
+        def make_hi1(g):
+            nc.vector.tensor_scalar(
+                out=hi1[g][:], in0=xh[g][:, :, 0], scalar1=BOUNDS[MID], scalar2=None, op0=ALU.is_gt
+            )
+
+        sel = [keep.tile([P, L * P], F32, name="sel%d" % j) for j in range(NT)]
+        xg = [keep.tile([P, L * P * 4], BF16, name="xg%d" % j, align_bytes=64) for j in range(NT)]
+        xq = [keep.tile([P, L * P], U32, name="xq%d" % j, align_bytes=64) for j in range(NT)]
+        xs = [keep.tile([P, L * P], U8, name="xs%d" % j, align_bytes=64) for j in range(NT)]
+        pts = {}
+
+        def sel_and_transpose(j):
+            g, i = where[j]
+            nc.vector.tensor_scalar(
+                out=sel[j][:], in0=colv[:], scalar1=lo[g][:, i : i + 1],
+                scalar2=None, op0=ALU.is_equal,
+            )
+            words = xh[g][:].rearrange("p j d -> p (j d)").bitcast(F32)
+            for half in range(2):
+                pt = psum.tile(
+                    [P, 2, 2, P], F32, tag="bank%d" % T_BANKS[j][half], name="pt%d_%d" % (j, half)
+                )
+                pts[(j, half)] = pt
+                for u in range(2):
+                    c0 = i * (D // 2) + u
+                    for li in range(2):
+                        c = 2 * half + li
+                        nc.tensor.transpose(
+                            out=pt[:, li, u, :],
+                            in_=words[:, c0 : c0 + 2 * P - 1 : 2],
+                            identity=sel[j][:, c * P : (c + 1) * P],
+                        )
+
+        def copy_out(j):
+            dst = xg[j][:].bitcast(F32).rearrange("p (l t u) -> p l t u", l=L, u=2)
+            for half in range(2):
+                nc.scalar.copy(
+                    out=dst[:, 2 * half : 2 * half + 2, :, :],
+                    in_=pts[(j, half)][:].rearrange("p l u t -> p l t u"),
+                )
+
+        def quant_x(j):
+            nc.vector.quantize_mx(out=xq[j][:].bitcast(FP8X4), scales=xs[j][:], in_=xg[j][:])
+
+        wg = [keep.tile([P, F, 4], BF16, name="wg%d" % k, align_bytes=64) for k in range(NE)]
+        wq = [keep.tile([P, F], U32, name="wq%d" % k, align_bytes=64) for k in range(NE)]
+        ws = [keep.tile([P, F], U8, name="ws%d" % k, align_bytes=64) for k in range(NE)]
+
+        def regroup(k):
+            fv = FV[k]
+            if fv > 0:
+                nc.vector.tensor_copy(
+                    out=wg[k][:, 0:fv, :].rearrange("p (c i) t -> p c t i", i=4),
+                    in_=raw[k][:, :, 0:fv].rearrange("p t (c i) -> p c t i", i=4),
+                )
+            if fv < F:
+                nc.scalar.copy(
+                    out=wg[k][:, fv:F, :].rearrange("p (c i) t -> p c t i", i=4),
+                    in_=raw[k][:, :, fv:F].rearrange("p t (c i) -> p c t i", i=4),
+                )
+
+        def quant_w(k):
+            nc.vector.quantize_mx(
+                out=wq[k][:].bitcast(FP8X4), scales=ws[k][:],
+                in_=wg[k][:].rearrange("p f t -> p (f t)"),
+            )
+
+        acc = {}
+
+        def mx(j, k):
+            h, c = k // L, k % L
+            if c == 0:
+                acc[(j, h)] = psum.tile([P, F], F32, tag="bank%d" % j, name="acc%d_%d" % (j, h))
+            nc.tensor.matmul_mx(
+                out=acc[(j, h)][:],
+                lhsT=xq[j][:, c * P : (c + 1) * P].bitcast(FP8X4),
+                lhsT_scale=xs[j][:, c * P : (c + 1) * P],
+                rhs=wq[k][:].bitcast(FP8X4),
+                rhs_scale=ws[k][:],
+                start=(c == 0),
+                stop=(c == L - 1),
+            )
+
+        part = [keep.tile([P, F], F32, name="part%d" % j) for j in range(NT)]
+        res = [keep.tile([P, F], F32, name="res%d" % j) for j in range(NT)]
+
+        def first_half(j):
+            g, i = where[j]
+            nc.scalar.activation(
+                out=part[j][:], in_=acc[(j, 0)][:], func=ACT.Copy, scale=cmp[g][:, i, nb - 1 : nb]
+            )
+
+        def second_half(j):
+            g, i = where[j]
+            nc.vector.scalar_tensor_tensor(
+                out=res[j][:], in0=acc[(j, 1)][:], scalar=hi1[g][:, i : i + 1],
+                in1=part[j][:], op0=ALU.mult, op1=ALU.add,
+            )
+            nc.sync.dma_start(out=o_v[:, j, :], in_=res[j][:])
+
+        def last_tile_half(half, bank):
+            j = NT - 1
+            g, i = where[j]
+            cols = slice(half * (F // 2), (half + 1) * (F // 2))
+            ps = psum.tile([P, F // 2], F32, tag="bank%d" % bank, name="last%d" % half)
+            for c in range(L):
+                nc.tensor.matmul_mx(
+                    out=ps[:],
+                    lhsT=xq[j][:, c * P : (c + 1) * P].bitcast(FP8X4),
+                    lhsT_scale=xs[j][:, c * P : (c + 1) * P],
+                    rhs=wq[L + c][:, cols].bitcast(FP8X4),
+                    rhs_scale=ws[L + c][:, cols],
+                    start=(c == 0),
+                    stop=(c == L - 1),
+                )
+            nc.vector.scalar_tensor_tensor(
+                out=res[j][:, cols], in0=ps[:], scalar=hi1[g][:, i : i + 1],
+                in1=part[j][:, cols], op0=ALU.mult, op1=ALU.add,
+            )
+            nc.sync.dma_start(out=o_v[:, j, cols], in_=res[j][:, cols])
+
+        quantised_x = []
+        quantised_w = []
+        bank_free = [0, 1, 2, 3]
+        issued = []
+
+        def sweep():
+            for j in quantised_x:
+                if j in bank_free:
+                    for k in quantised_w:
+                        if (j, k) not in issued:
+                            issued.append((j, k))
+                            mx(j, k)
+
+        bucket_cmp(0)
+        bucket_sum(0)
+        sel_and_transpose(0)
+        sel_and_transpose(1)
+        regroup(0)
+        bucket_cmp(1)
+        copy_out(0)
+        quant_w(0)
+        quantised_w.append(0)
+        bucket_sum(1)
+        bucket_cmp(2)
+        sel_and_transpose(2)
+        bucket_sum(2)
+        sel_and_transpose(3)
+        pending = []
+        for j in range(NT):
+            if j > 0:
+                copy_out(j)
+            if 2 <= j < NT - 2:
+                sel_and_transpose(j + 2)
+            if j >= NT - 2:
+                bank_free.extend(T_BANKS[j])
+                sweep()
+            for k in pending:
+                quant_w(k)
+                quantised_w.append(k)
+                sweep()
+            pending = []
+            for k in W_AFTER.get(j, ()):
+                regroup(k)
+                pending.append(k)
+            quant_x(j)
+            quantised_x.append(j)
+            sweep()
+        regroup(4)
+        regroup(5)
+        for j in range(4):
+            first_half(j)
+        quant_w(4)
+        quant_w(5)
+        regroup(6)
+        regroup(7)
+        first_half(4)
+        quant_w(6)
+        first_half(5)
+        quant_w(7)
+        first_half(6)
+        first_half(7)
+        for g in range(len(X_GROUPS)):
+            make_hi1(g)
+        for k in (4, 5):
+            for j in range(4):
+                mx(j, k)
+        for j in range(4):
+            mx(j, 6)
+            mx(j, 7)
+            second_half(j)
+        for j in range(4, NT - 1):
+            for k in range(L, NE):
+                mx(j, k)
+            second_half(j)
+        for half, bank in enumerate((NT - 1, 0)):
+            last_tile_half(half, bank)

@@ -112,25 +112,30 @@ def tile_dispatchbyvariable_pa_kernel(tc, x, W, out):
         xs = [keep.tile([P, L * P], U8, name="xs%d" % j, align_bytes=64) for j in range(NT)]
         pts = {}
 
+        xw = [keep.tile([P, 2, P], F32, name="xw%d" % j) for j in range(NT)]
+
+        def reorder(j):
+            g, i = where[j]
+            words = xh[g][:, i, :].bitcast(F32)
+            nc.vector.tensor_copy(out=xw[j][:], in_=words.rearrange("p (q u) -> p u q", u=2))
+
         def sel_and_transpose(j):
             g, i = where[j]
             nc.vector.tensor_scalar(
                 out=sel[j][:], in0=colv[:], scalar1=lo[g][:, i : i + 1],
                 scalar2=None, op0=ALU.is_equal,
             )
-            words = xh[g][:].rearrange("p j d -> p (j d)").bitcast(F32)
             for half in range(2):
                 pt = psum.tile(
                     [P, 2, 2, P], F32, tag="bank%d" % T_BANKS[j][half], name="pt%d_%d" % (j, half)
                 )
                 pts[(j, half)] = pt
                 for u in range(2):
-                    c0 = i * (D // 2) + u
                     for li in range(2):
                         c = 2 * half + li
                         nc.tensor.transpose(
                             out=pt[:, li, u, :],
-                            in_=words[:, c0 : c0 + 2 * P - 1 : 2],
+                            in_=xw[j][:, u, :],
                             identity=sel[j][:, c * P : (c + 1) * P],
                         )
 
@@ -237,10 +242,13 @@ def tile_dispatchbyvariable_pa_kernel(tc, x, W, out):
 
         bucket_cmp(0)
         bucket_sum(0)
+        reorder(0)
         sel_and_transpose(0)
+        reorder(1)
         sel_and_transpose(1)
         regroup(0)
         bucket_cmp(1)
+        reorder(2)
         copy_out(0)
         quant_w(0)
         quantised_w.append(0)
@@ -248,12 +256,14 @@ def tile_dispatchbyvariable_pa_kernel(tc, x, W, out):
         bucket_cmp(2)
         sel_and_transpose(2)
         bucket_sum(2)
+        reorder(3)
         sel_and_transpose(3)
         pending = []
         for j in range(NT):
             if j > 0:
                 copy_out(j)
             if 2 <= j < NT - 2:
+                reorder(j + 2)
                 sel_and_transpose(j + 2)
             if j >= NT - 2:
                 bank_free.extend(T_BANKS[j])

@@ -69,6 +69,8 @@ def tile_dispatchbyvariable_pa_kernel(tc, x, W, out):
             col_i[:], pattern=[[1, L * P]], base=0, channel_multiplier=-1,
             allow_small_or_imprecise_dtypes=True,
         )
+        zeros = keep.tile([P, F], BF16, name="zeros")
+        nc.vector.memset(zeros[:], 0.0)
         bins = keep.tile([P, nb - 1], F32, name="bins")
         for i, b in enumerate(BOUNDS[:MID] + BOUNDS[MID + 1 :]):
             nc.vector.memset(bins[:, i : i + 1], b)
@@ -111,6 +113,12 @@ def tile_dispatchbyvariable_pa_kernel(tc, x, W, out):
         xq = [keep.tile([P, L * P], U32, name="xq%d" % j, align_bytes=64) for j in range(NT)]
         xs = [keep.tile([P, L * P], U8, name="xs%d" % j, align_bytes=64) for j in range(NT)]
         pts = {}
+
+        idle_bank = psum.tile([P, F], F32, tag="bank7", name="idle_bank")
+
+        def keep_clock(n):
+            for i in range(n):
+                nc.tensor.matmul(out=idle_bank[:], lhsT=zeros[:, 0:P], rhs=zeros[:], start=True, stop=True)
 
         xw = [keep.tile([P, 2, P], F32, name="xw%d" % j) for j in range(NT)]
 
@@ -240,12 +248,14 @@ def tile_dispatchbyvariable_pa_kernel(tc, x, W, out):
                             issued.append((j, k))
                             mx(j, k)
 
+        keep_clock(6)
         bucket_cmp(0)
         bucket_sum(0)
         reorder(0)
         sel_and_transpose(0)
         reorder(1)
         sel_and_transpose(1)
+        keep_clock(2)
         regroup(0)
         bucket_cmp(1)
         reorder(2)
@@ -255,6 +265,7 @@ def tile_dispatchbyvariable_pa_kernel(tc, x, W, out):
         bucket_sum(1)
         bucket_cmp(2)
         sel_and_transpose(2)
+        keep_clock(1)
         bucket_sum(2)
         reorder(3)
         sel_and_transpose(3)

@@ -109,9 +109,9 @@ def tile_dispatchbyvariable_pa_kernel(tc, x, W, out):
             )
 
         sel = [keep.tile([P, L * P], F32, name="sel%d" % j) for j in range(NT)]
-        xg = [keep.tile([P, L * P * 4], BF16, name="xg%d" % j, align_bytes=64) for j in range(NT)]
-        xq = [keep.tile([P, L * P], U32, name="xq%d" % j, align_bytes=64) for j in range(NT)]
-        xs = [keep.tile([P, L * P], U8, name="xs%d" % j, align_bytes=64) for j in range(NT)]
+        xg = [keep.tile([P, L * P * 4], BF16, name="xg%d" % j, align_bytes=256) for j in range(NT)]
+        xq = [keep.tile([P, L * P], U32, name="xq%d" % j, align_bytes=256) for j in range(NT)]
+        xs = [keep.tile([P, L * P], U8, name="xs%d" % j, align_bytes=256) for j in range(NT)]
         pts = {}
 
         idle_bank = psum.tile([P, F], F32, tag="bank7", name="idle_bank")
@@ -158,9 +158,9 @@ def tile_dispatchbyvariable_pa_kernel(tc, x, W, out):
         def quant_x(j):
             nc.vector.quantize_mx(out=xq[j][:].bitcast(FP8X4), scales=xs[j][:], in_=xg[j][:])
 
-        wg = [keep.tile([P, F, 4], BF16, name="wg%d" % k, align_bytes=64) for k in range(NE)]
-        wq = [keep.tile([P, F], U32, name="wq%d" % k, align_bytes=64) for k in range(NE)]
-        ws = [keep.tile([P, F], U8, name="ws%d" % k, align_bytes=64) for k in range(NE)]
+        wg = [keep.tile([P, F, 4], BF16, name="wg%d" % k, align_bytes=256) for k in range(NE)]
+        wq = [keep.tile([P, F], U32, name="wq%d" % k, align_bytes=256) for k in range(NE)]
+        ws = [keep.tile([P, F], U8, name="ws%d" % k, align_bytes=256) for k in range(NE)]
 
         def regroup(k):
             fv = FV[k]

@@ -18,162 +18,189 @@ NT = 8
 D = 512
 F = 512
 NE = 8
-L = 4
-BOUNDS = (-1.5, -1.0, -0.5, 0.0, 0.5, 1.0, 1.5)
+LOADS = (("x", 0), ("w", 0), ("x", 1), ("x", 2), ("w", 1), ("w", 2), ("w", 3), ("w", 4), ("w", 5), ("w", 6), ("w", 7))
+GROUPS = ((0, 1), (2, 3), (4, 5, 6, 7))
+COPIES = (2, 2, 4)
+UP = {2: (-1.5, -0.5, 0.5, 1.5), 4: (-1.5, -1.0, -0.5, 0.5, 1.0, 1.5)}
+DOWN = {2: (-1.0, 0.0, 1.0), 4: (0.0, 0.0, 0.0)}
+FV = (256, 128, 448, 384, 256, 512, 0, 64)
 MID = 3
-FV = [352,352,352,352,352,352,352,352]
-X_GROUPS = ((0, 1), (2, 3), (4, 5, 6, 7))
-T_BANKS = ((0, 1), (2, 3), (4, 5), (6, 7), (4, 5), (6, 7), (4, 5), (6, 7))
-W_AFTER = {2: (1,), 4: (2,), 5: (3,)}
-PINNED = True
 
 
 def tile_dispatchbyvariable_pa_kernel(tc, x, W, out):
     nc = tc.nc
     x_v = x.flatten_outer_dims().rearrange("(p j) d -> p j d", j=NT)
     o_v = out.flatten_outer_dims().rearrange("(p j) f -> p j f", j=NT)
-    nb = len(BOUNDS)
     where = {}
-    for g, tiles in enumerate(X_GROUPS):
+    for g, tiles in enumerate(GROUPS):
         for i, j in enumerate(tiles):
             where[j] = (g, i)
 
     with ExitStack() as ctx:
-        if PINNED:
-            ctx.enter_context(tc.manual_schedule())
+        ctx.enter_context(tc.manual_schedule())
         keep = ctx.enter_context(tc.tile_pool(name="keep", bufs=1))
         psum = ctx.enter_context(tc.psum_pool(name="psum", bufs=1))
 
-        xh = [keep.tile([P, len(t), D], BF16, name="xh%d" % g) for g, t in enumerate(X_GROUPS)]
+        xh = [keep.tile([P, len(t), D], BF16, name="xh%d" % g) for g, t in enumerate(GROUPS)]
         raw = [keep.tile([P, 4, F], BF16, name="raw%d" % k) for k in range(NE)]
+        for what, n in LOADS:
+            if what == "x":
+                t = GROUPS[n]
+                nc.sync.dma_start(out=xh[n][:], in_=x_v[:, t[0] : t[0] + len(t), :])
+            else:
+                nc.sync.dma_start(
+                    out=raw[n][:].rearrange("p t f -> p (t f)"),
+                    in_=W[n].rearrange("(p t) f -> p (t f)", t=4),
+                )
 
-        def load_x(g):
-            t = X_GROUPS[g]
-            nc.sync.dma_start(out=xh[g][:], in_=x_v[:, t[0] : t[0] + len(t), :])
-
-        def load_w(k):
-            nc.sync.dma_start(
-                out=raw[k][:].rearrange("p t f -> p (t f)"),
-                in_=W[k].rearrange("(p t) f -> p (t f)", t=4),
-            )
-
-        load_x(0)
-        load_w(0)
-        load_x(1)
-        load_x(2)
-        for k in range(1, NE):
-            load_w(k)
-
-        col_i = keep.tile([P, L * P], F32, name="col_i")
+        col_i = keep.tile([P, 4 * P], F32, name="col_i")
         nc.gpsimd.iota(
-            col_i[:], pattern=[[1, L * P]], base=0, channel_multiplier=-1,
+            col_i[:], pattern=[[1, 4 * P]], base=0, channel_multiplier=-1,
             allow_small_or_imprecise_dtypes=True,
         )
-        zeros = keep.tile([P, F], BF16, name="zeros")
-        nc.vector.memset(zeros[:], 0.0)
-        bins = keep.tile([P, nb - 1], F32, name="bins")
-        for i, b in enumerate(BOUNDS[:MID] + BOUNDS[MID + 1 :]):
-            nc.vector.memset(bins[:, i : i + 1], b)
+        bins = {}
+        for L in (2, 4):
+            edges = UP[L] + DOWN[L]
+            bins[L] = keep.tile([P, len(edges)], F32, name="bins%d" % L)
+            for i, b in enumerate(edges):
+                nc.vector.memset(bins[L][:, i : i + 1], b)
         warm = keep.tile([P, 1], F32, name="warm")
-        nc.scalar.activation(out=warm[:], in_=bins[:, 0:1], func=ACT.Copy)
-        colv = keep.tile([P, L * P], F32, name="colv")
+        nc.scalar.activation(out=warm[:], in_=bins[2][:, 0:1], func=ACT.Copy)
+        ge = []
+        for g, t in enumerate(GROUPS):
+            R = NE // COPIES[g]
+            ge.append(keep.tile([P, len(t), R + 1], F32, name="ge%d" % g))
+            nc.vector.memset(ge[g][:], 0.0)
+            nc.vector.memset(ge[g][:, :, 0:1], 1.0)
+        colv = keep.tile([P, 4 * P], F32, name="colv")
         nc.vector.tensor_scalar(
             out=colv[:], in0=col_i[:], scalar1=1.0 / P, scalar2=float(MID), op0=ALU.mult, op1=ALU.add
         )
 
-        ncmp = nb - 1 + MID
-        cmp = [keep.tile([P, len(t), ncmp], F32, name="cmp%d" % g) for g, t in enumerate(X_GROUPS)]
-        lo = [keep.tile([P, len(t)], F32, name="lo%d" % g) for g, t in enumerate(X_GROUPS)]
-        hi1 = [keep.tile([P, len(t)], F32, name="hi1_%d" % g) for g, t in enumerate(X_GROUPS)]
+        cmp = []
+        cls = []
+        hot = []
+        xw = []
+        for g, t in enumerate(GROUPS):
+            L = COPIES[g]
+            n = len(t)
+            cmp.append(keep.tile([P, n, len(UP[L]) + MID], F32, name="cmp%d" % g))
+            cls.append(keep.tile([P, n], F32, name="cls%d" % g))
+            hot.append(keep.tile([P, n, NE // L], F32, name="hot%d" % g))
+            xw.append(keep.tile([P, n, 2, P], F32, name="xw%d" % g))
 
-        def bucket_cmp(g):
-            n = len(X_GROUPS[g])
+        def compare(g):
+            L = COPIES[g]
+            n = len(GROUPS[g])
+            nu = len(UP[L])
+            for a, b, op in ((0, nu, ALU.is_gt), (nu, nu + MID, ALU.is_le)):
+                nc.vector.tensor_tensor(
+                    out=cmp[g][:, :, a:b],
+                    in0=xh[g][:, :, 0:1].to_broadcast([P, n, b - a]),
+                    in1=bins[L][:, a:b].unsqueeze(1).to_broadcast([P, n, b - a]),
+                    op=op,
+                )
+
+        def count(g):
+            nc.vector.tensor_reduce(out=cls[g][:], in_=cmp[g][:], axis=AX.X, op=ALU.add)
+
+        def edges(g):
+            L = COPIES[g]
+            R = NE // L
+            n = len(GROUPS[g])
+            nu = len(UP[L])
             nc.vector.tensor_tensor(
-                out=cmp[g][:, :, 0 : nb - 1],
-                in0=xh[g][:, :, 0:1].to_broadcast([P, n, nb - 1]),
-                in1=bins[:].unsqueeze(1).to_broadcast([P, n, nb - 1]),
+                out=ge[g][:, :, 1:R],
+                in0=xh[g][:, :, 0:1].to_broadcast([P, n, R - 1]),
+                in1=bins[L][:, nu : nu + R - 1].unsqueeze(1).to_broadcast([P, n, R - 1]),
                 op=ALU.is_gt,
             )
-            nc.vector.tensor_scalar(
-                out=cmp[g][:, :, nb - 1 : ncmp],
-                in0=xh[g][:, :, 0:1].to_broadcast([P, n, MID]),
-                scalar1=BOUNDS[MID], scalar2=0.0, op0=ALU.is_gt, op1=ALU.is_equal,
+
+        def rounds(g):
+            R = NE // COPIES[g]
+            nc.vector.tensor_tensor(
+                out=hot[g][:], in0=ge[g][:, :, 0:R], in1=ge[g][:, :, 1 : R + 1], op=ALU.subtract
             )
 
-        def bucket_sum(g):
-            nc.vector.tensor_reduce(out=lo[g][:], in_=cmp[g][:], axis=AX.X, op=ALU.add)
+        def reorder(g, a, b, on_scalar=False):
+            src = xh[g][:].rearrange("p j d -> p (j d)").bitcast(F32)
+            src = src.rearrange("p (j q u) -> p j u q", u=2, q=P)
+            if on_scalar:
+                nc.scalar.copy(out=xw[g][:, a:b], in_=src[:, a:b])
+            else:
+                nc.vector.tensor_copy(out=xw[g][:, a:b], in_=src[:, a:b])
 
-        def make_hi1(g):
-            nc.vector.tensor_scalar(
-                out=hi1[g][:], in0=xh[g][:, :, 0], scalar1=BOUNDS[MID], scalar2=None, op0=ALU.is_gt
-            )
+        free = list(range(8))
+        holder = {}
 
-        sel = [keep.tile([P, L * P], F32, name="sel%d" % j) for j in range(NT)]
-        xg = [keep.tile([P, L * P * 4], BF16, name="xg%d" % j, align_bytes=256) for j in range(NT)]
-        xq = [keep.tile([P, L * P], U32, name="xq%d" % j, align_bytes=256) for j in range(NT)]
-        xs = [keep.tile([P, L * P], U8, name="xs%d" % j, align_bytes=256) for j in range(NT)]
+        def take(key):
+            b = free[0]
+            free.remove(b)
+            holder[key] = b
+            return "bank%d" % b
+
+        def give(key):
+            free.append(holder[key])
+
+        sel = {}
         pts = {}
+        xg = {}
+        xq = {}
+        xs = {}
 
-        idle_bank = psum.tile([P, F], F32, tag="bank7", name="idle_bank")
-
-        def keep_clock(n):
-            for i in range(n):
-                nc.tensor.matmul(out=idle_bank[:], lhsT=zeros[:, 0:P], rhs=zeros[:], start=True, stop=True)
-
-        xw = [keep.tile([P, 2, P], F32, name="xw%d" % j) for j in range(NT)]
-
-        def reorder(j):
+        def select(j):
             g, i = where[j]
-            words = xh[g][:, i, :].bitcast(F32)
-            nc.vector.tensor_copy(out=xw[j][:], in_=words.rearrange("p (q u) -> p u q", u=2))
-
-        def sel_and_transpose(j):
-            g, i = where[j]
+            L = COPIES[g]
+            sel[j] = keep.tile([P, L * P], F32, name="sel%d" % j)
             nc.vector.tensor_scalar(
-                out=sel[j][:], in0=colv[:], scalar1=lo[g][:, i : i + 1],
-                scalar2=None, op0=ALU.is_equal,
+                out=sel[j][:], in0=colv[:, 0 : L * P],
+                scalar1=cls[g][:, i : i + 1], scalar2=None, op0=ALU.is_equal,
             )
-            for half in range(2):
-                pt = psum.tile(
-                    [P, 2, 2, P], F32, tag="bank%d" % T_BANKS[j][half], name="pt%d_%d" % (j, half)
-                )
-                pts[(j, half)] = pt
-                for u in range(2):
-                    for li in range(2):
-                        c = 2 * half + li
-                        nc.tensor.transpose(
-                            out=pt[:, li, u, :],
-                            in_=xw[j][:, u, :],
-                            identity=sel[j][:, c * P : (c + 1) * P],
-                        )
 
-        def copy_out(j):
+        def transposes(j):
+            g, i = where[j]
+            L = COPIES[g]
+            for h in range(L // 2):
+                pts[(j, h)] = psum.tile([P, 2, 2, P], F32, tag=take(("t", j, h)), name="pt%d_%d" % (j, h))
+                for u in range(2):
+                    for c in range(2):
+                        s = (2 * h + c) * P
+                        nc.tensor.transpose(
+                            out=pts[(j, h)][:, c, u, :],
+                            in_=xw[g][:, i, u, :],
+                            identity=sel[j][:, s : s + P],
+                        )
+            xg[j] = keep.tile([P, L * P * 4], BF16, name="xg%d" % j, align_bytes=256)
+
+        def copy_x(j, h, on_vector=False):
+            L = COPIES[where[j][0]]
             dst = xg[j][:].bitcast(F32).rearrange("p (l t u) -> p l t u", l=L, u=2)
-            for half in range(2):
-                nc.scalar.copy(
-                    out=dst[:, 2 * half : 2 * half + 2, :, :],
-                    in_=pts[(j, half)][:].rearrange("p l u t -> p l t u"),
-                )
+            dst = dst[:, 2 * h : 2 * h + 2, :, :]
+            src = pts[(j, h)][:].rearrange("p l u t -> p l t u")
+            if on_vector:
+                nc.vector.tensor_copy(out=dst, in_=src)
+            else:
+                nc.scalar.copy(out=dst, in_=src)
+            give(("t", j, h))
 
         def quant_x(j):
+            L = COPIES[where[j][0]]
+            xq[j] = keep.tile([P, L * P], U32, name="xq%d" % j, align_bytes=256)
+            xs[j] = keep.tile([P, L * P], U8, name="xs%d" % j, align_bytes=256)
             nc.vector.quantize_mx(out=xq[j][:].bitcast(FP8X4), scales=xs[j][:], in_=xg[j][:])
 
         wg = [keep.tile([P, F, 4], BF16, name="wg%d" % k, align_bytes=256) for k in range(NE)]
         wq = [keep.tile([P, F], U32, name="wq%d" % k, align_bytes=256) for k in range(NE)]
         ws = [keep.tile([P, F], U8, name="ws%d" % k, align_bytes=256) for k in range(NE)]
 
-        def regroup(k):
-            fv = FV[k]
-            if fv > 0:
-                nc.vector.tensor_copy(
-                    out=wg[k][:, 0:fv, :].rearrange("p (c i) t -> p c t i", i=4),
-                    in_=raw[k][:, :, 0:fv].rearrange("p t (c i) -> p c t i", i=4),
-                )
-            if fv < F:
-                nc.scalar.copy(
-                    out=wg[k][:, fv:F, :].rearrange("p (c i) t -> p c t i", i=4),
-                    in_=raw[k][:, :, fv:F].rearrange("p t (c i) -> p c t i", i=4),
-                )
+        def regroup(k, engine):
+            cols = slice(0, FV[k]) if engine == "v" else slice(FV[k], F)
+            dst = wg[k][:, cols, :].rearrange("p (c i) t -> p c t i", i=4)
+            src = raw[k][:, :, cols].rearrange("p t (c i) -> p c t i", i=4)
+            if engine == "v":
+                nc.vector.tensor_copy(out=dst, in_=src)
+            else:
+                nc.scalar.copy(out=dst, in_=src)
 
         def quant_w(k):
             nc.vector.quantize_mx(
@@ -182,140 +209,218 @@ def tile_dispatchbyvariable_pa_kernel(tc, x, W, out):
             )
 
         acc = {}
+        count_of = {}
+        part = {}
 
-        def mx(j, k):
-            h, c = k // L, k % L
-            if c == 0:
-                acc[(j, h)] = psum.tile([P, F], F32, tag="bank%d" % j, name="acc%d_%d" % (j, h))
+        def mx(j, k, dst=None, cols=slice(0, F)):
+            L = COPIES[where[j][0]]
+            r, c = k // L, k % L
+            n = count_of.get((j, r, cols.start), 0)
+            count_of[(j, r, cols.start)] = n + 1
+            if dst is None:
+                if n == 0:
+                    acc[(j, r)] = psum.tile([P, F], F32, tag=take(("a", j, r)), name="acc%d_%d" % (j, r))
+                dst = acc[(j, r)][:]
             nc.tensor.matmul_mx(
-                out=acc[(j, h)][:],
+                out=dst,
                 lhsT=xq[j][:, c * P : (c + 1) * P].bitcast(FP8X4),
                 lhsT_scale=xs[j][:, c * P : (c + 1) * P],
-                rhs=wq[k][:].bitcast(FP8X4),
-                rhs_scale=ws[k][:],
-                start=(c == 0),
-                stop=(c == L - 1),
+                rhs=wq[k][:, cols].bitcast(FP8X4),
+                rhs_scale=ws[k][:, cols],
+                start=(n == 0),
+                stop=(n == L - 1),
             )
 
-        part = [keep.tile([P, F], F32, name="part%d" % j) for j in range(NT)]
-        res = [keep.tile([P, F], F32, name="res%d" % j) for j in range(NT)]
-
-        def first_half(j):
+        def read(j, r, src=None, cols=slice(0, F), on_vector=False):
             g, i = where[j]
-            nc.scalar.activation(
-                out=part[j][:], in_=acc[(j, 0)][:], func=ACT.Copy, scale=cmp[g][:, i, nb - 1 : nb]
-            )
-
-        def second_half(j):
-            g, i = where[j]
-            nc.vector.scalar_tensor_tensor(
-                out=res[j][:], in0=acc[(j, 1)][:], scalar=hi1[g][:, i : i + 1],
-                in1=part[j][:], op0=ALU.mult, op1=ALU.add,
-            )
-            nc.sync.dma_start(out=o_v[:, j, :], in_=res[j][:])
-
-        def last_tile_half(half, bank):
-            j = NT - 1
-            g, i = where[j]
-            cols = slice(half * (F // 2), (half + 1) * (F // 2))
-            ps = psum.tile([P, F // 2], F32, tag="bank%d" % bank, name="last%d" % half)
-            for c in range(L):
-                nc.tensor.matmul_mx(
-                    out=ps[:],
-                    lhsT=xq[j][:, c * P : (c + 1) * P].bitcast(FP8X4),
-                    lhsT_scale=xs[j][:, c * P : (c + 1) * P],
-                    rhs=wq[L + c][:, cols].bitcast(FP8X4),
-                    rhs_scale=ws[L + c][:, cols],
-                    start=(c == 0),
-                    stop=(c == L - 1),
+            if (j, r) not in part:
+                part[(j, r)] = keep.tile([P, F], F32, name="part%d_%d" % (j, r))
+            dst = part[(j, r)][:, cols]
+            mask = hot[g][:, i, r : r + 1]
+            if src is None:
+                src = acc[(j, r)][:]
+                give(("a", j, r))
+            if r > 0:
+                nc.vector.scalar_tensor_tensor(
+                    out=dst, in0=src, scalar=mask, in1=part[(j, r - 1)][:, cols],
+                    op0=ALU.mult, op1=ALU.add,
                 )
-            nc.vector.scalar_tensor_tensor(
-                out=res[j][:, cols], in0=ps[:], scalar=hi1[g][:, i : i + 1],
-                in1=part[j][:, cols], op0=ALU.mult, op1=ALU.add,
-            )
-            nc.sync.dma_start(out=o_v[:, j, cols], in_=res[j][:, cols])
+            elif on_vector:
+                nc.vector.tensor_scalar(out=dst, in0=src, scalar1=mask, scalar2=None, op0=ALU.mult)
+            else:
+                nc.scalar.activation(out=dst, in_=src, func=ACT.Copy, scale=mask)
+            if r == NE // COPIES[g] - 1:
+                nc.sync.dma_start(out=o_v[:, j, cols], in_=dst)
 
-        quantised_x = []
-        quantised_w = []
-        bank_free = [0, 1, 2, 3]
-        issued = []
+        def last_tile(j):
+            L = COPIES[where[j][0]]
+            r = NE // L - 1
+            for half in range(2):
+                cols = slice(half * (F // 2), (half + 1) * (F // 2))
+                ps = psum.tile([P, F // 2], F32, tag=take(("l", half)), name="last%d" % half)
+                for k in range(r * L, NE):
+                    mx(j, k, ps[:], cols)
+                read(j, r, ps[:], cols)
 
-        def sweep():
-            for j in quantised_x:
-                if j in bank_free:
-                    for k in quantised_w:
-                        if (j, k) not in issued:
-                            issued.append((j, k))
-                            mx(j, k)
-
-        keep_clock(6)
-        bucket_cmp(0)
-        bucket_sum(0)
-        reorder(0)
-        sel_and_transpose(0)
-        reorder(1)
-        sel_and_transpose(1)
-        keep_clock(2)
-        regroup(0)
-        bucket_cmp(1)
-        reorder(2)
-        copy_out(0)
+        compare(0)
+        reorder(*where[0], where[0][1] + 1)
+        count(0)
+        edges(0)
+        select(0)
+        rounds(0)
+        transposes(0)
+        reorder(*where[1], where[1][1] + 1)
+        select(1)
+        transposes(1)
+        regroup(0, "v")
+        regroup(0, "s")
+        compare(1)
+        reorder(*where[2], where[2][1] + 1)
+        count(1)
+        edges(1)
+        select(2)
+        rounds(1)
+        transposes(2)
+        copy_x(0, 0)
+        reorder(*where[3], where[3][1] + 1)
+        select(3)
+        transposes(3)
         quant_w(0)
-        quantised_w.append(0)
-        bucket_sum(1)
-        bucket_cmp(2)
-        sel_and_transpose(2)
-        keep_clock(1)
-        bucket_sum(2)
-        reorder(3)
-        sel_and_transpose(3)
-        pending = []
-        for j in range(NT):
-            if j > 0:
-                copy_out(j)
-            if 2 <= j < NT - 2:
-                reorder(j + 2)
-                sel_and_transpose(j + 2)
-            if j >= NT - 2:
-                bank_free.extend(T_BANKS[j])
-                sweep()
-            for k in pending:
-                quant_w(k)
-                quantised_w.append(k)
-                sweep()
-            pending = []
-            for k in W_AFTER.get(j, ()):
-                regroup(k)
-                pending.append(k)
-            quant_x(j)
-            quantised_x.append(j)
-            sweep()
-        regroup(4)
-        regroup(5)
-        for j in range(4):
-            first_half(j)
+        copy_x(1, 0)
+        quant_x(0)
+        copy_x(2, 0)
+        mx(0, 0)
+        compare(2)
+        reorder(*where[4], where[4][1] + 1)
+        count(2)
+        edges(2)
+        select(4)
+        rounds(2)
+        transposes(4)
+        quant_x(1)
+        copy_x(3, 0)
+        mx(1, 0)
+        reorder(*where[5], where[5][1] + 1)
+        select(5)
+        transposes(5)
+        quant_x(2)
+        regroup(1, "v")
+        regroup(1, "s")
+        reorder(*where[6], where[6][1] + 1)
+        select(6)
+        transposes(6)
+        quant_x(3)
+        copy_x(4, 0)
+        copy_x(4, 1)
+        quant_w(1)
+        copy_x(5, 0)
+        copy_x(5, 1)
+        mx(0, 1)
+        mx(1, 1)
+        reorder(*where[7], where[7][1] + 1)
+        select(7)
+        transposes(7)
+        quant_x(4)
+        copy_x(6, 0)
+        copy_x(6, 1)
+        mx(2, 0)
+        mx(2, 1)
+        mx(3, 0)
+        mx(3, 1)
+        mx(4, 0)
+        mx(4, 1)
+        quant_x(5)
+        regroup(2, "v")
+        regroup(2, "s")
+        mx(5, 0)
+        mx(5, 1)
+        quant_x(6)
+        copy_x(7, 0)
+        copy_x(7, 1)
+        read(0, 0)
+        read(1, 0)
+        mx(6, 0)
+        mx(6, 1)
+        quant_w(2)
+        regroup(3, "v")
+        regroup(3, "s")
+        read(2, 0)
+        read(3, 0)
+        mx(0, 2)
+        mx(1, 2)
+        mx(2, 2)
+        mx(3, 2)
+        mx(4, 2)
+        mx(5, 2)
+        mx(6, 2)
+        quant_x(7)
+        regroup(4, "v")
+        regroup(4, "s")
+        mx(7, 0)
+        mx(7, 1)
+        mx(7, 2)
+        quant_w(3)
+        regroup(5, "v")
+        mx(0, 3)
+        mx(1, 3)
+        mx(2, 3)
+        mx(3, 3)
+        mx(4, 3)
+        mx(5, 3)
+        mx(6, 3)
+        mx(7, 3)
         quant_w(4)
+        regroup(6, "s")
         quant_w(5)
-        regroup(6)
-        regroup(7)
-        first_half(4)
+        regroup(7, "v")
+        regroup(7, "s")
+        read(0, 1)
+        read(1, 1)
+        read(2, 1)
+        read(3, 1)
+        mx(0, 4)
+        mx(0, 5)
+        mx(1, 4)
+        mx(1, 5)
+        mx(2, 4)
+        mx(2, 5)
+        mx(3, 4)
+        mx(3, 5)
         quant_w(6)
-        first_half(5)
+        read(4, 0)
+        read(5, 0)
+        read(6, 0)
+        read(7, 0)
+        mx(4, 4)
+        mx(4, 5)
+        mx(4, 6)
+        mx(5, 4)
+        mx(5, 5)
+        mx(5, 6)
         quant_w(7)
-        first_half(6)
-        first_half(7)
-        for g in range(len(X_GROUPS)):
-            make_hi1(g)
-        for k in (4, 5):
-            for j in range(4):
-                mx(j, k)
-        for j in range(4):
-            mx(j, 6)
-            mx(j, 7)
-            second_half(j)
-        for j in range(4, NT - 1):
-            for k in range(L, NE):
-                mx(j, k)
-            second_half(j)
-        for half, bank in enumerate((NT - 1, 0)):
-            last_tile_half(half, bank)
+        read(0, 2)
+        read(1, 2)
+        read(2, 2)
+        read(3, 2)
+        mx(0, 6)
+        mx(0, 7)
+        mx(1, 6)
+        mx(1, 7)
+        mx(2, 6)
+        mx(2, 7)
+        mx(3, 6)
+        mx(3, 7)
+        mx(4, 7)
+        mx(5, 7)
+        mx(6, 4)
+        mx(6, 5)
+        mx(6, 6)
+        mx(6, 7)
+        read(0, 3)
+        read(1, 3)
+        read(2, 3)
+        read(3, 3)
+        read(4, 1)
+        read(5, 1)
+        read(6, 1)
+        last_tile(7)

@@ -18,13 +18,20 @@ NT = 8
 D = 512
 F = 512
 NE = 8
-LOADS = (("x", 0), ("w", 0), ("x", 1), ("x", 2), ("w", 1), ("w", 2), ("w", 3), ("w", 4), ("w", 5), ("w", 6), ("w", 7))
+BOUNDS = (-1.5, -1.0, -0.5, 0.0, 0.5, 1.0, 1.5)
+ORDER = (0, 4, 2, 6, 1, 5, 3, 7)
 GROUPS = ((0, 1), (2, 3), (4, 5, 6, 7))
-COPIES = (2, 2, 4)
-UP = {2: (-1.5, -0.5, 0.5, 1.5), 4: (-1.5, -1.0, -0.5, 0.5, 1.0, 1.5)}
-DOWN = {2: (-1.0, 0.0, 1.0), 4: (0.0, 0.0, 0.0)}
-FV = (256, 128, 448, 384, 256, 512, 0, 64)
-MID = 3
+COPIES = (4, 2, 4)
+EDGES = {2: (0.0,), 4: (-1.0, 0.0, 1.0)}
+LOADS = (("x", 0), ("w", 0), ("x", 1), ("x", 2), ("w", 1), ("w", 2), ("w", 3), ("w", 4), ("w", 5), ("w", 6), ("w", 7))
+ITEMS = (("w", 0), ("x", 0), ("x", 1), ("w", 1), ("x", 2), ("x", 3), ("x", 4), ("x", 5), ("w", 2), ("x", 6), ("w", 3), ("x", 7), ("w", 4), ("w", 5), ("w", 6), ("w", 7))
+FV = (256, 256, 384, 384, 384, 0, 256, 512)
+REORDER = ("s", "n", "v")
+VECTOR_COPIES = ()
+VECTOR_PARTS = ()
+CLASSES, FRONT, COPY, REGROUP_V, REGROUP_S, PART, SUM = 6, 5, 3, 2, 2, 3, 2
+SPARE = 1
+MAX_LAST = 3
 
 
 def tile_dispatchbyvariable_pa_kernel(tc, x, W, out):
@@ -41,8 +48,8 @@ def tile_dispatchbyvariable_pa_kernel(tc, x, W, out):
         keep = ctx.enter_context(tc.tile_pool(name="keep", bufs=1))
         psum = ctx.enter_context(tc.psum_pool(name="psum", bufs=1))
 
-        xh = [keep.tile([P, len(t), D], BF16, name="xh%d" % g) for g, t in enumerate(GROUPS)]
-        raw = [keep.tile([P, 4, F], BF16, name="raw%d" % k) for k in range(NE)]
+        xh = [keep.tile([P, len(t), D], BF16, name="xh%d" % g, align_bytes=256) for g, t in enumerate(GROUPS)]
+        raw = [keep.tile([P, 4, F], BF16, name="raw%d" % k, align_bytes=256) for k in range(NE)]
         for what, n in LOADS:
             if what == "x":
                 t = GROUPS[n]
@@ -50,7 +57,7 @@ def tile_dispatchbyvariable_pa_kernel(tc, x, W, out):
             else:
                 nc.sync.dma_start(
                     out=raw[n][:].rearrange("p t f -> p (t f)"),
-                    in_=W[n].rearrange("(p t) f -> p (t f)", t=4),
+                    in_=W[ORDER[n]].rearrange("(p t) f -> p (t f)", t=4),
                 )
 
         col_i = keep.tile([P, 4 * P], F32, name="col_i")
@@ -58,77 +65,79 @@ def tile_dispatchbyvariable_pa_kernel(tc, x, W, out):
             col_i[:], pattern=[[1, 4 * P]], base=0, channel_multiplier=-1,
             allow_small_or_imprecise_dtypes=True,
         )
-        bins = {}
-        for L in (2, 4):
-            edges = UP[L] + DOWN[L]
-            bins[L] = keep.tile([P, len(edges)], F32, name="bins%d" % L)
-            for i, b in enumerate(edges):
-                nc.vector.memset(bins[L][:, i : i + 1], b)
+        edges = keep.tile([P, 3], F32, name="edges")
+        for i, b in enumerate(EDGES[4]):
+            nc.vector.memset(edges[:, i : i + 1], b)
         warm = keep.tile([P, 1], F32, name="warm")
-        nc.scalar.activation(out=warm[:], in_=bins[2][:, 0:1], func=ACT.Copy)
-        ge = []
+        nc.scalar.activation(out=warm[:], in_=edges[:, 0:1], func=ACT.Copy)
+        bins = keep.tile([P, len(BOUNDS)], F32, name="bins")
+        for i, b in enumerate(BOUNDS):
+            nc.vector.memset(bins[:, i : i + 1], b)
+        above = []
         for g, t in enumerate(GROUPS):
-            R = NE // COPIES[g]
-            ge.append(keep.tile([P, len(t), R + 1], F32, name="ge%d" % g))
-            nc.vector.memset(ge[g][:], 0.0)
-            nc.vector.memset(ge[g][:, :, 0:1], 1.0)
+            above.append(keep.tile([P, len(t), NE + 1], F32, name="above%d" % g))
+            nc.gpsimd.memset(above[g][:], 0.0)
+            nc.gpsimd.memset(above[g][:, :, 0:1], 1.0)
         colv = keep.tile([P, 4 * P], F32, name="colv")
-        nc.vector.tensor_scalar(
-            out=colv[:], in0=col_i[:], scalar1=1.0 / P, scalar2=float(MID), op0=ALU.mult, op1=ALU.add
-        )
+        nc.vector.tensor_scalar(out=colv[:], in0=col_i[:], scalar1=1.0 / P, scalar2=None, op0=ALU.mult)
 
-        cmp = []
-        cls = []
-        hot = []
-        xw = []
-        for g, t in enumerate(GROUPS):
-            L = COPIES[g]
-            n = len(t)
-            cmp.append(keep.tile([P, n, len(UP[L]) + MID], F32, name="cmp%d" % g))
-            cls.append(keep.tile([P, n], F32, name="cls%d" % g))
-            hot.append(keep.tile([P, n, NE // L], F32, name="hot%d" % g))
-            xw.append(keep.tile([P, n, 2, P], F32, name="xw%d" % g))
+        cls = [keep.tile([P, len(t)], F32, name="cls%d" % g) for g, t in enumerate(GROUPS)]
+        hot = {}
+        xw = {}
 
-        def compare(g):
-            L = COPIES[g]
+        def classes(g):
             n = len(GROUPS[g])
-            nu = len(UP[L])
-            for a, b, op in ((0, nu, ALU.is_gt), (nu, nu + MID, ALU.is_le)):
-                nc.vector.tensor_tensor(
-                    out=cmp[g][:, :, a:b],
-                    in0=xh[g][:, :, 0:1].to_broadcast([P, n, b - a]),
-                    in1=bins[L][:, a:b].unsqueeze(1).to_broadcast([P, n, b - a]),
-                    op=op,
+            L = COPIES[g]
+            if L == 2:
+                nc.vector.tensor_scalar(
+                    out=cls[g][:], in0=xh[g][:, :, 0], scalar1=EDGES[2][0], scalar2=None, op0=ALU.is_gt
                 )
+                reorder(g)
+            else:
+                m = len(EDGES[L])
+                cmp = keep.tile([P, n, m], F32, name="cmp%d" % g)
+                nc.vector.tensor_tensor(
+                    out=cmp[:],
+                    in0=xh[g][:, :, 0:1].to_broadcast([P, n, m]),
+                    in1=edges[:].unsqueeze(1).to_broadcast([P, n, m]),
+                    op=ALU.is_gt,
+                )
+                reorder(g)
+                nc.vector.tensor_reduce(out=cls[g][:], in_=cmp[:], axis=AX.X, op=ALU.add)
 
-        def count(g):
-            nc.vector.tensor_reduce(out=cls[g][:], in_=cmp[g][:], axis=AX.X, op=ALU.add)
-
-        def edges(g):
-            L = COPIES[g]
-            R = NE // L
+        def masks(g):
             n = len(GROUPS[g])
-            nu = len(UP[L])
-            nc.vector.tensor_tensor(
-                out=ge[g][:, :, 1:R],
-                in0=xh[g][:, :, 0:1].to_broadcast([P, n, R - 1]),
-                in1=bins[L][:, nu : nu + R - 1].unsqueeze(1).to_broadcast([P, n, R - 1]),
-                op=ALU.is_gt,
-            )
-
-        def rounds(g):
             R = NE // COPIES[g]
-            nc.vector.tensor_tensor(
-                out=hot[g][:], in0=ge[g][:, :, 0:R], in1=ge[g][:, :, 1 : R + 1], op=ALU.subtract
+            for i in range(n):
+                nc.gpsimd.tensor_scalar(
+                    out=above[g][:, i, 1:NE], in0=bins[:], scalar1=xh[g][:, i, 0:1],
+                    scalar2=None, op0=ALU.is_lt,
+                )
+            width = NE
+            now = keep.tile([P, n, width], F32, name="hot%d_%d" % (g, width))
+            nc.gpsimd.tensor_tensor(
+                out=now[:], in0=above[g][:, :, 0:NE], in1=above[g][:, :, 1 : NE + 1], op=ALU.subtract
             )
+            while width > R:
+                width //= 2
+                half = keep.tile([P, n, width], F32, name="hot%d_%d" % (g, width))
+                nc.gpsimd.tensor_tensor(
+                    out=half[:], in0=now[:, :, 0:width], in1=now[:, :, width : 2 * width], op=ALU.add
+                )
+                now = half
+            hot[g] = now
 
-        def reorder(g, a, b, on_scalar=False):
+        def reorder(g):
+            if REORDER[g] == "n":
+                return
+            n = len(GROUPS[g])
+            xw[g] = keep.tile([P, n, 2, P], F32, name="xw%d" % g)
             src = xh[g][:].rearrange("p j d -> p (j d)").bitcast(F32)
             src = src.rearrange("p (j q u) -> p j u q", u=2, q=P)
-            if on_scalar:
-                nc.scalar.copy(out=xw[g][:, a:b], in_=src[:, a:b])
+            if REORDER[g] == "s":
+                nc.scalar.copy(out=xw[g][:], in_=src)
             else:
-                nc.vector.tensor_copy(out=xw[g][:, a:b], in_=src[:, a:b])
+                nc.vector.tensor_copy(out=xw[g][:], in_=src)
 
         free = list(range(8))
         holder = {}
@@ -165,262 +174,181 @@ def tile_dispatchbyvariable_pa_kernel(tc, x, W, out):
                 for u in range(2):
                     for c in range(2):
                         s = (2 * h + c) * P
+                        if g in xw:
+                            words = xw[g][:, i, u, :]
+                        else:
+                            words = xh[g][:, i, :].bitcast(F32)[:, u : 2 * P - 1 + u : 2]
                         nc.tensor.transpose(
-                            out=pts[(j, h)][:, c, u, :],
-                            in_=xw[g][:, i, u, :],
-                            identity=sel[j][:, s : s + P],
+                            out=pts[(j, h)][:, c, u, :], in_=words, identity=sel[j][:, s : s + P]
                         )
             xg[j] = keep.tile([P, L * P * 4], BF16, name="xg%d" % j, align_bytes=256)
 
-        def copy_x(j, h, on_vector=False):
+        def copy_x(j):
             L = COPIES[where[j][0]]
             dst = xg[j][:].bitcast(F32).rearrange("p (l t u) -> p l t u", l=L, u=2)
-            dst = dst[:, 2 * h : 2 * h + 2, :, :]
-            src = pts[(j, h)][:].rearrange("p l u t -> p l t u")
-            if on_vector:
-                nc.vector.tensor_copy(out=dst, in_=src)
-            else:
-                nc.scalar.copy(out=dst, in_=src)
-            give(("t", j, h))
-
-        def quant_x(j):
-            L = COPIES[where[j][0]]
-            xq[j] = keep.tile([P, L * P], U32, name="xq%d" % j, align_bytes=256)
-            xs[j] = keep.tile([P, L * P], U8, name="xs%d" % j, align_bytes=256)
-            nc.vector.quantize_mx(out=xq[j][:].bitcast(FP8X4), scales=xs[j][:], in_=xg[j][:])
+            for h in range(L // 2):
+                src = pts[(j, h)][:].rearrange("p l u t -> p l t u")
+                if (j, h) in VECTOR_COPIES:
+                    nc.vector.tensor_copy(out=dst[:, 2 * h : 2 * h + 2, :, :], in_=src)
+                else:
+                    nc.scalar.copy(out=dst[:, 2 * h : 2 * h + 2, :, :], in_=src)
+                give(("t", j, h))
 
         wg = [keep.tile([P, F, 4], BF16, name="wg%d" % k, align_bytes=256) for k in range(NE)]
         wq = [keep.tile([P, F], U32, name="wq%d" % k, align_bytes=256) for k in range(NE)]
         ws = [keep.tile([P, F], U8, name="ws%d" % k, align_bytes=256) for k in range(NE)]
 
-        def regroup(k, engine):
-            cols = slice(0, FV[k]) if engine == "v" else slice(FV[k], F)
-            dst = wg[k][:, cols, :].rearrange("p (c i) t -> p c t i", i=4)
-            src = raw[k][:, :, cols].rearrange("p t (c i) -> p c t i", i=4)
-            if engine == "v":
-                nc.vector.tensor_copy(out=dst, in_=src)
-            else:
-                nc.scalar.copy(out=dst, in_=src)
-
-        def quant_w(k):
-            nc.vector.quantize_mx(
-                out=wq[k][:].bitcast(FP8X4), scales=ws[k][:],
-                in_=wg[k][:].rearrange("p f t -> p (f t)"),
+        def regroup_views(k, cols):
+            return (
+                wg[k][:, cols, :].rearrange("p (c i) t -> p c t i", i=4),
+                raw[k][:, :, cols].rearrange("p t (c i) -> p c t i", i=4),
             )
 
-        acc = {}
-        count_of = {}
-        part = {}
+        def regroup_vector(k):
+            if FV[k] > 0:
+                dst, src = regroup_views(k, slice(0, FV[k]))
+                nc.vector.tensor_copy(out=dst, in_=src)
 
-        def mx(j, k, dst=None, cols=slice(0, F)):
-            L = COPIES[where[j][0]]
-            r, c = k // L, k % L
-            n = count_of.get((j, r, cols.start), 0)
-            count_of[(j, r, cols.start)] = n + 1
-            if dst is None:
-                if n == 0:
-                    acc[(j, r)] = psum.tile([P, F], F32, tag=take(("a", j, r)), name="acc%d_%d" % (j, r))
-                dst = acc[(j, r)][:]
+        def regroup_scalar(k):
+            if FV[k] < F:
+                dst, src = regroup_views(k, slice(FV[k], F))
+                nc.scalar.copy(out=dst, in_=src)
+
+        ready_x = []
+        ready_w = []
+
+        def quantise(item):
+            what, n = item
+            if what == "x":
+                L = COPIES[where[n][0]]
+                xq[n] = keep.tile([P, L * P], U32, name="xq%d" % n, align_bytes=256)
+                xs[n] = keep.tile([P, L * P], U8, name="xs%d" % n, align_bytes=256)
+                nc.vector.quantize_mx(out=xq[n][:].bitcast(FP8X4), scales=xs[n][:], in_=xg[n][:])
+                ready_x.append(n)
+            else:
+                nc.vector.quantize_mx(
+                    out=wq[n][:].bitcast(FP8X4), scales=ws[n][:],
+                    in_=wg[n][:].rearrange("p f t -> p (f t)"),
+                )
+                ready_w.append(n)
+
+        acc = {}
+        used = {}
+        part = {}
+        waiting = []
+
+        def mx(j, k, dst, cols, first, last):
+            c = ORDER[k] // (NE // COPIES[where[j][0]])
             nc.tensor.matmul_mx(
                 out=dst,
                 lhsT=xq[j][:, c * P : (c + 1) * P].bitcast(FP8X4),
                 lhsT_scale=xs[j][:, c * P : (c + 1) * P],
                 rhs=wq[k][:, cols].bitcast(FP8X4),
                 rhs_scale=ws[k][:, cols],
-                start=(n == 0),
-                stop=(n == L - 1),
+                start=first,
+                stop=last,
             )
 
-        def read(j, r, src=None, cols=slice(0, F), on_vector=False):
+        def read(j, r, src, cols):
             g, i = where[j]
+            R = NE // COPIES[g]
             if (j, r) not in part:
                 part[(j, r)] = keep.tile([P, F], F32, name="part%d_%d" % (j, r))
             dst = part[(j, r)][:, cols]
-            mask = hot[g][:, i, r : r + 1]
-            if src is None:
-                src = acc[(j, r)][:]
-                give(("a", j, r))
+            m = ORDER[r * COPIES[g]] % R
+            mask = hot[g][:, i, m : m + 1]
             if r > 0:
                 nc.vector.scalar_tensor_tensor(
                     out=dst, in0=src, scalar=mask, in1=part[(j, r - 1)][:, cols],
                     op0=ALU.mult, op1=ALU.add,
                 )
-            elif on_vector:
+            elif j in VECTOR_PARTS:
                 nc.vector.tensor_scalar(out=dst, in0=src, scalar1=mask, scalar2=None, op0=ALU.mult)
             else:
                 nc.scalar.activation(out=dst, in_=src, func=ACT.Copy, scale=mask)
-            if r == NE // COPIES[g] - 1:
+            if r == R - 1:
                 nc.sync.dma_start(out=o_v[:, j, cols], in_=dst)
 
-        def last_tile(j):
-            L = COPIES[where[j][0]]
-            r = NE // L - 1
-            for half in range(2):
-                cols = slice(half * (F // 2), (half + 1) * (F // 2))
-                ps = psum.tile([P, F // 2], F32, tag=take(("l", half)), name="last%d" % half)
-                for k in range(r * L, NE):
-                    mx(j, k, ps[:], cols)
-                read(j, r, ps[:], cols)
+        def reads(n):
+            for kind in (0, 1):
+                for q in [q for q in waiting if min(q[2], 1) == kind]:
+                    step, j, r = q
+                    if n is None or step + (SUM if r > 0 else PART) <= n:
+                        read(j, r, acc[(j, r)][:], slice(0, F))
+                        give(("a", j, r))
+                        waiting.remove(q)
 
-        compare(0)
-        reorder(*where[0], where[0][1] + 1)
-        count(0)
-        edges(0)
-        select(0)
-        rounds(0)
-        transposes(0)
-        reorder(*where[1], where[1][1] + 1)
-        select(1)
-        transposes(1)
-        regroup(0, "v")
-        regroup(0, "s")
-        compare(1)
-        reorder(*where[2], where[2][1] + 1)
-        count(1)
-        edges(1)
-        select(2)
-        rounds(1)
-        transposes(2)
-        copy_x(0, 0)
-        reorder(*where[3], where[3][1] + 1)
-        select(3)
-        transposes(3)
-        quant_w(0)
-        copy_x(1, 0)
-        quant_x(0)
-        copy_x(2, 0)
-        mx(0, 0)
-        compare(2)
-        reorder(*where[4], where[4][1] + 1)
-        count(2)
-        edges(2)
-        select(4)
-        rounds(2)
-        transposes(4)
-        quant_x(1)
-        copy_x(3, 0)
-        mx(1, 0)
-        reorder(*where[5], where[5][1] + 1)
-        select(5)
-        transposes(5)
-        quant_x(2)
-        regroup(1, "v")
-        regroup(1, "s")
-        reorder(*where[6], where[6][1] + 1)
-        select(6)
-        transposes(6)
-        quant_x(3)
-        copy_x(4, 0)
-        copy_x(4, 1)
-        quant_w(1)
-        copy_x(5, 0)
-        copy_x(5, 1)
-        mx(0, 1)
-        mx(1, 1)
-        reorder(*where[7], where[7][1] + 1)
-        select(7)
-        transposes(7)
-        quant_x(4)
-        copy_x(6, 0)
-        copy_x(6, 1)
-        mx(2, 0)
-        mx(2, 1)
-        mx(3, 0)
-        mx(3, 1)
-        mx(4, 0)
-        mx(4, 1)
-        quant_x(5)
-        regroup(2, "v")
-        regroup(2, "s")
-        mx(5, 0)
-        mx(5, 1)
-        quant_x(6)
-        copy_x(7, 0)
-        copy_x(7, 1)
-        read(0, 0)
-        read(1, 0)
-        mx(6, 0)
-        mx(6, 1)
-        quant_w(2)
-        regroup(3, "v")
-        regroup(3, "s")
-        read(2, 0)
-        read(3, 0)
-        mx(0, 2)
-        mx(1, 2)
-        mx(2, 2)
-        mx(3, 2)
-        mx(4, 2)
-        mx(5, 2)
-        mx(6, 2)
-        quant_x(7)
-        regroup(4, "v")
-        regroup(4, "s")
-        mx(7, 0)
-        mx(7, 1)
-        mx(7, 2)
-        quant_w(3)
-        regroup(5, "v")
-        mx(0, 3)
-        mx(1, 3)
-        mx(2, 3)
-        mx(3, 3)
-        mx(4, 3)
-        mx(5, 3)
-        mx(6, 3)
-        mx(7, 3)
-        quant_w(4)
-        regroup(6, "s")
-        quant_w(5)
-        regroup(7, "v")
-        regroup(7, "s")
-        read(0, 1)
-        read(1, 1)
-        read(2, 1)
-        read(3, 1)
-        mx(0, 4)
-        mx(0, 5)
-        mx(1, 4)
-        mx(1, 5)
-        mx(2, 4)
-        mx(2, 5)
-        mx(3, 4)
-        mx(3, 5)
-        quant_w(6)
-        read(4, 0)
-        read(5, 0)
-        read(6, 0)
-        read(7, 0)
-        mx(4, 4)
-        mx(4, 5)
-        mx(4, 6)
-        mx(5, 4)
-        mx(5, 5)
-        mx(5, 6)
-        quant_w(7)
-        read(0, 2)
-        read(1, 2)
-        read(2, 2)
-        read(3, 2)
-        mx(0, 6)
-        mx(0, 7)
-        mx(1, 6)
-        mx(1, 7)
-        mx(2, 6)
-        mx(2, 7)
-        mx(3, 6)
-        mx(3, 7)
-        mx(4, 7)
-        mx(5, 7)
-        mx(6, 4)
-        mx(6, 5)
-        mx(6, 6)
-        mx(6, 7)
-        read(0, 3)
-        read(1, 3)
-        read(2, 3)
-        read(3, 3)
-        read(4, 1)
-        read(5, 1)
-        read(6, 1)
-        last_tile(7)
+        last = NT - 1
+
+        def passes(n):
+            for j in sorted(ready_x):
+                L = COPIES[where[j][0]]
+                R = NE // L
+                for r in range(R):
+                    if j == last and r == R - 1:
+                        continue
+                    ks = [k for k in range(r * L, r * L + L) if k in ready_w and (j, k) not in used]
+                    if not ks:
+                        continue
+                    if (j, r) not in acc:
+                        if r > 0 and (j, r - 1) not in part:
+                            break
+                        if len(free) <= (SPARE if len(pts) < sum(COPIES[where[q][0]] // 2 for q in range(NT)) else 0):
+                            continue
+                        open_last = [
+                            q for q in acc
+                            if q[1] == NE // COPIES[where[q[0]][0]] - 1
+                            and len([k for k in range(NE) if (q[0], k) in used and k // COPIES[where[q[0]][0]] == q[1]])
+                            < COPIES[where[q[0]][0]]
+                        ]
+                        if r == R - 1 and len(open_last) >= MAX_LAST and len(ks) < L:
+                            continue
+                        acc[(j, r)] = psum.tile([P, F], F32, tag=take(("a", j, r)), name="acc%d_%d" % (j, r))
+                    for k in ks:
+                        n_used = len([q for q in range(r * L, r * L + L) if (j, q) in used])
+                        mx(j, k, acc[(j, r)][:], slice(0, F), n_used == 0, n_used == L - 1)
+                        used[(j, k)] = True
+                    if len([q for q in range(r * L, r * L + L) if (j, q) in used]) == L:
+                        waiting.append((n, j, r))
+
+        begun = []
+
+        def at(n):
+            return ITEMS[n] if 0 <= n < len(ITEMS) else None
+
+        for n in range(-8, len(ITEMS)):
+            item = at(n + FRONT)
+            if item and item[0] == "x":
+                select(item[1])
+            item = at(n + CLASSES)
+            if item and item[0] == "x" and where[item[1]][0] not in begun:
+                begun.append(where[item[1]][0])
+                classes(where[item[1]][0])
+                masks(where[item[1]][0])
+            if 0 <= n:
+                quantise(ITEMS[n])
+            item = at(n + FRONT)
+            if item and item[0] == "x":
+                transposes(item[1])
+            item = at(n + REGROUP_V)
+            if item and item[0] == "w":
+                regroup_vector(item[1])
+            reads(n)
+            item = at(n + REGROUP_S)
+            if item and item[0] == "w":
+                regroup_scalar(item[1])
+            item = at(n + COPY)
+            if item and item[0] == "x":
+                copy_x(item[1])
+            if n >= 0:
+                passes(n)
+        while waiting or len(used) < NT * NE - COPIES[where[last][0]]:
+            reads(None)
+            passes(len(ITEMS))
+        L = COPIES[where[last][0]]
+        for half in range(2):
+            cols = slice(half * (F // 2), (half + 1) * (F // 2))
+            ps = psum.tile([P, F // 2], F32, tag=take(("l", half)), name="last%d" % half)
+            for k in range(NE - L, NE):
+                mx(last, k, ps[:], cols, k == NE - L, k == NE - 1)
+            read(last, NE // L - 1, ps[:], cols)

@@ -18,18 +18,17 @@ NT = 8
 D = 512
 F = 512
 NE = 8
-BOUNDS = (-1.5, -1.0, -0.5, 0.0, 0.5, 1.0, 1.5)
-ORDER = (0, 4, 2, 6, 1, 5, 3, 7)
+UP = {2: (-1.5, -0.5, 0.5, 1.5), 4: (-1.5, -1.0, -0.5, 0.5, 1.0, 1.5)}
+DOWN = {2: (-1.0, 0.0, 1.0), 4: (0.0, 0.0, 0.0)}
 GROUPS = ((0, 1), (2, 3), (4, 5, 6, 7))
 COPIES = (4, 2, 4)
-EDGES = {2: (0.0,), 4: (-1.0, 0.0, 1.0)}
 LOADS = (("x", 0), ("w", 0), ("x", 1), ("x", 2), ("w", 1), ("w", 2), ("w", 3), ("w", 4), ("w", 5), ("w", 6), ("w", 7))
 ITEMS = (("w", 0), ("x", 0), ("x", 1), ("w", 1), ("x", 2), ("x", 3), ("x", 4), ("x", 5), ("w", 2), ("x", 6), ("w", 3), ("x", 7), ("w", 4), ("w", 5), ("w", 6), ("w", 7))
 FV = (256, 256, 384, 384, 384, 0, 256, 512)
 REORDER = ("s", "n", "v")
 VECTOR_COPIES = ()
 VECTOR_PARTS = ()
-CLASSES, FRONT, COPY, REGROUP_V, REGROUP_S, PART, SUM = 6, 5, 3, 2, 2, 3, 2
+CLASSES, MASKS, FRONT, COPY, REGROUP_V, REGROUP_S, PART, SUM = 6, 1, 5, 3, 2, 2, 3, 2
 SPARE = 1
 MAX_LAST = 3
 
@@ -57,7 +56,7 @@ def tile_dispatchbyvariable_pa_kernel(tc, x, W, out):
             else:
                 nc.sync.dma_start(
                     out=raw[n][:].rearrange("p t f -> p (t f)"),
-                    in_=W[ORDER[n]].rearrange("(p t) f -> p (t f)", t=4),
+                    in_=W[n].rearrange("(p t) f -> p (t f)", t=4),
                 )
 
         col_i = keep.tile([P, 4 * P], F32, name="col_i")
@@ -65,67 +64,48 @@ def tile_dispatchbyvariable_pa_kernel(tc, x, W, out):
             col_i[:], pattern=[[1, 4 * P]], base=0, channel_multiplier=-1,
             allow_small_or_imprecise_dtypes=True,
         )
-        edges = keep.tile([P, 3], F32, name="edges")
-        for i, b in enumerate(EDGES[4]):
-            nc.vector.memset(edges[:, i : i + 1], b)
-        warm = keep.tile([P, 1], F32, name="warm")
-        nc.scalar.activation(out=warm[:], in_=edges[:, 0:1], func=ACT.Copy)
-        bins = keep.tile([P, len(BOUNDS)], F32, name="bins")
-        for i, b in enumerate(BOUNDS):
-            nc.vector.memset(bins[:, i : i + 1], b)
-        above = []
+        bins = {}
+        for L in (2, 4):
+            edges = UP[L] + DOWN[L]
+            bins[L] = keep.tile([P, len(edges)], F32, name="bins%d" % L)
+            for i, b in enumerate(edges):
+                nc.vector.memset(bins[L][:, i : i + 1], b)
+            if L == 2:
+                warm = keep.tile([P, 1], F32, name="warm")
+                nc.scalar.activation(out=warm[:], in_=bins[2][:, 0:1], func=ACT.Copy)
+        cmp = []
         for g, t in enumerate(GROUPS):
-            above.append(keep.tile([P, len(t), NE + 1], F32, name="above%d" % g))
-            nc.gpsimd.memset(above[g][:], 0.0)
-            nc.gpsimd.memset(above[g][:, :, 0:1], 1.0)
+            cmp.append(keep.tile([P, len(t), 5 + len(UP[COPIES[g]])], F32, name="cmp%d" % g))
+            nc.vector.memset(cmp[g][:, :, 0:1], 0.0)
+            nc.vector.memset(cmp[g][:, :, 4:5], 1.0)
         colv = keep.tile([P, 4 * P], F32, name="colv")
-        nc.vector.tensor_scalar(out=colv[:], in0=col_i[:], scalar1=1.0 / P, scalar2=None, op0=ALU.mult)
+        nc.vector.tensor_scalar(out=colv[:], in0=col_i[:], scalar1=1.0 / P, scalar2=4.0, op0=ALU.mult, op1=ALU.add)
 
         cls = [keep.tile([P, len(t)], F32, name="cls%d" % g) for g, t in enumerate(GROUPS)]
         hot = {}
         xw = {}
 
-        def classes(g):
+        def against(dst, g, a, b, op):
             n = len(GROUPS[g])
-            L = COPIES[g]
-            if L == 2:
-                nc.vector.tensor_scalar(
-                    out=cls[g][:], in0=xh[g][:, :, 0], scalar1=EDGES[2][0], scalar2=None, op0=ALU.is_gt
-                )
-                reorder(g)
-            else:
-                m = len(EDGES[L])
-                cmp = keep.tile([P, n, m], F32, name="cmp%d" % g)
-                nc.vector.tensor_tensor(
-                    out=cmp[:],
-                    in0=xh[g][:, :, 0:1].to_broadcast([P, n, m]),
-                    in1=edges[:].unsqueeze(1).to_broadcast([P, n, m]),
-                    op=ALU.is_gt,
-                )
-                reorder(g)
-                nc.vector.tensor_reduce(out=cls[g][:], in_=cmp[:], axis=AX.X, op=ALU.add)
+            nc.vector.tensor_tensor(
+                out=dst,
+                in0=xh[g][:, :, 0:1].to_broadcast([P, n, b - a]),
+                in1=bins[COPIES[g]][:, a:b].unsqueeze(1).to_broadcast([P, n, b - a]),
+                op=op,
+            )
+
+        def classes(g):
+            up = len(UP[COPIES[g]])
+            against(cmp[g][:, :, 1:4], g, up, up + 3, ALU.is_le)
+            against(cmp[g][:, :, 5 : 5 + up], g, 0, up, ALU.is_gt)
+            reorder(g)
+            nc.vector.tensor_reduce(out=cls[g][:], in_=cmp[g][:], axis=AX.X, op=ALU.add)
 
         def masks(g):
-            n = len(GROUPS[g])
-            R = NE // COPIES[g]
-            for i in range(n):
-                nc.gpsimd.tensor_scalar(
-                    out=above[g][:, i, 1:NE], in0=bins[:], scalar1=xh[g][:, i, 0:1],
-                    scalar2=None, op0=ALU.is_lt,
-                )
-            width = NE
-            now = keep.tile([P, n, width], F32, name="hot%d_%d" % (g, width))
-            nc.gpsimd.tensor_tensor(
-                out=now[:], in0=above[g][:, :, 0:NE], in1=above[g][:, :, 1 : NE + 1], op=ALU.subtract
+            hot[g] = keep.tile([P, len(GROUPS[g]), 4], F32, name="hot%d" % g)
+            nc.vector.tensor_tensor(
+                out=hot[g][:], in0=cmp[g][:, :, 1:5], in1=cmp[g][:, :, 0:4], op=ALU.subtract
             )
-            while width > R:
-                width //= 2
-                half = keep.tile([P, n, width], F32, name="hot%d_%d" % (g, width))
-                nc.gpsimd.tensor_tensor(
-                    out=half[:], in0=now[:, :, 0:width], in1=now[:, :, width : 2 * width], op=ALU.add
-                )
-                now = half
-            hot[g] = now
 
         def reorder(g):
             if REORDER[g] == "n":
@@ -238,7 +218,7 @@ def tile_dispatchbyvariable_pa_kernel(tc, x, W, out):
         waiting = []
 
         def mx(j, k, dst, cols, first, last):
-            c = ORDER[k] // (NE // COPIES[where[j][0]])
+            c = k % COPIES[where[j][0]]
             nc.tensor.matmul_mx(
                 out=dst,
                 lhsT=xq[j][:, c * P : (c + 1) * P].bitcast(FP8X4),
@@ -255,7 +235,7 @@ def tile_dispatchbyvariable_pa_kernel(tc, x, W, out):
             if (j, r) not in part:
                 part[(j, r)] = keep.tile([P, F], F32, name="part%d_%d" % (j, r))
             dst = part[(j, r)][:, cols]
-            m = ORDER[r * COPIES[g]] % R
+            m = r * 3 // (R - 1)
             mask = hot[g][:, i, m : m + 1]
             if r > 0:
                 nc.vector.scalar_tensor_tensor(
@@ -312,6 +292,7 @@ def tile_dispatchbyvariable_pa_kernel(tc, x, W, out):
                         waiting.append((n, j, r))
 
         begun = []
+        masked = []
 
         def at(n):
             return ITEMS[n] if 0 <= n < len(ITEMS) else None
@@ -324,7 +305,6 @@ def tile_dispatchbyvariable_pa_kernel(tc, x, W, out):
             if item and item[0] == "x" and where[item[1]][0] not in begun:
                 begun.append(where[item[1]][0])
                 classes(where[item[1]][0])
-                masks(where[item[1]][0])
             if 0 <= n:
                 quantise(ITEMS[n])
             item = at(n + FRONT)
@@ -340,6 +320,10 @@ def tile_dispatchbyvariable_pa_kernel(tc, x, W, out):
             item = at(n + COPY)
             if item and item[0] == "x":
                 copy_x(item[1])
+            item = at(n + MASKS)
+            if item and item[0] == "x" and where[item[1]][0] not in masked:
+                masked.append(where[item[1]][0])
+                masks(where[item[1]][0])
             if n >= 0:
                 passes(n)
         while waiting or len(used) < NT * NE - COPIES[where[last][0]]:

from contextlib import ExitStack

import concourse.mybir as mybir

FLOPS = 2 * 1024 * 512 * 512 * 8

F32 = mybir.dt.float32
BF16 = mybir.dt.bfloat16
U32 = mybir.dt.uint32
U8 = mybir.dt.uint8
FP8X4 = mybir.dt.float8_e4m3fn_x4
ALU = mybir.AluOpType
ACT = mybir.ActivationFunctionType
AX = mybir.AxisListType

P = 128
NT = 8
D = 512
F = 512
NE = 8
UP = {2: (-1.5, -0.5, 0.5, 1.5), 4: (-1.5, -1.0, -0.5, 0.5, 1.0, 1.5)}
DOWN = {2: (-1.0, 0.0, 1.0), 4: (0.0, 0.0, 0.0)}
GROUPS = ((0, 1), (2, 3), (4, 5, 6, 7))
COPIES = (4, 2, 4)
LOADS = (("x", 0), ("w", 0), ("x", 1), ("x", 2), ("w", 1), ("w", 2), ("w", 3), ("w", 4), ("w", 5), ("w", 6), ("w", 7))
ITEMS = (("w", 0), ("x", 0), ("x", 1), ("w", 1), ("x", 2), ("x", 3), ("x", 4), ("x", 5), ("w", 2), ("x", 6), ("w", 3), ("x", 7), ("w", 4), ("w", 5), ("w", 6), ("w", 7))
FV = (256, 256, 384, 384, 384, 0, 256, 512)
REORDER = ("s", "n", "v")
VECTOR_COPIES = ()
VECTOR_PARTS = ()
CLASSES, MASKS, FRONT, COPY, REGROUP_V, REGROUP_S, PART, SUM = 6, 1, 5, 3, 2, 2, 3, 2
SPARE = 1
MAX_LAST = 3


def tile_dispatchbyvariable_pa_kernel(tc, x, W, out):
    nc = tc.nc
    x_v = x.flatten_outer_dims().rearrange("(p j) d -> p j d", j=NT)
    o_v = out.flatten_outer_dims().rearrange("(p j) f -> p j f", j=NT)
    where = {}
    for g, tiles in enumerate(GROUPS):
        for i, j in enumerate(tiles):
            where[j] = (g, i)

    with ExitStack() as ctx:
        ctx.enter_context(tc.manual_schedule())
        keep = ctx.enter_context(tc.tile_pool(name="keep", bufs=1))
        psum = ctx.enter_context(tc.psum_pool(name="psum", bufs=1))

        xh = [keep.tile([P, len(t), D], BF16, name="xh%d" % g, align_bytes=256) for g, t in enumerate(GROUPS)]
        raw = [keep.tile([P, 4, F], BF16, name="raw%d" % k, align_bytes=256) for k in range(NE)]
        for what, n in LOADS:
            if what == "x":
                t = GROUPS[n]
                nc.sync.dma_start(out=xh[n][:], in_=x_v[:, t[0] : t[0] + len(t), :])
            else:
                nc.sync.dma_start(
                    out=raw[n][:].rearrange("p t f -> p (t f)"),
                    in_=W[n].rearrange("(p t) f -> p (t f)", t=4),
                )

        col_i = keep.tile([P, 4 * P], F32, name="col_i")
        nc.gpsimd.iota(
            col_i[:], pattern=[[1, 4 * P]], base=0, channel_multiplier=-1,
            allow_small_or_imprecise_dtypes=True,
        )
        bins = {}
        for L in (2, 4):
            edges = UP[L] + DOWN[L]
            bins[L] = keep.tile([P, len(edges)], F32, name="bins%d" % L)
            for i, b in enumerate(edges):
                nc.vector.memset(bins[L][:, i : i + 1], b)
            if L == 2:
                warm = keep.tile([P, 1], F32, name="warm")
                nc.scalar.activation(out=warm[:], in_=bins[2][:, 0:1], func=ACT.Copy)
        cmp = []
        for g, t in enumerate(GROUPS):
            cmp.append(keep.tile([P, len(t), 5 + len(UP[COPIES[g]])], F32, name="cmp%d" % g))
            nc.vector.memset(cmp[g][:, :, 0:1], 0.0)
            nc.vector.memset(cmp[g][:, :, 4:5], 1.0)
        colv = keep.tile([P, 4 * P], F32, name="colv")
        nc.vector.tensor_scalar(out=colv[:], in0=col_i[:], scalar1=1.0 / P, scalar2=4.0, op0=ALU.mult, op1=ALU.add)

        cls = [keep.tile([P, len(t)], F32, name="cls%d" % g) for g, t in enumerate(GROUPS)]
        hot = {}
        xw = {}

        def against(dst, g, a, b, op):
            n = len(GROUPS[g])
            nc.vector.tensor_tensor(
                out=dst,
                in0=xh[g][:, :, 0:1].to_broadcast([P, n, b - a]),
                in1=bins[COPIES[g]][:, a:b].unsqueeze(1).to_broadcast([P, n, b - a]),
                op=op,
            )

        def classes(g):
            up = len(UP[COPIES[g]])
            against(cmp[g][:, :, 1:4], g, up, up + 3, ALU.is_le)
            against(cmp[g][:, :, 5 : 5 + up], g, 0, up, ALU.is_gt)
            reorder(g)
            nc.vector.tensor_reduce(out=cls[g][:], in_=cmp[g][:], axis=AX.X, op=ALU.add)

        def masks(g):
            hot[g] = keep.tile([P, len(GROUPS[g]), 4], F32, name="hot%d" % g)
            nc.vector.tensor_tensor(
                out=hot[g][:], in0=cmp[g][:, :, 1:5], in1=cmp[g][:, :, 0:4], op=ALU.subtract
            )

        def reorder(g):
            if REORDER[g] == "n":
                return
            n = len(GROUPS[g])
            xw[g] = keep.tile([P, n, 2, P], F32, name="xw%d" % g)
            src = xh[g][:].rearrange("p j d -> p (j d)").bitcast(F32)
            src = src.rearrange("p (j q u) -> p j u q", u=2, q=P)
            if REORDER[g] == "s":
                nc.scalar.copy(out=xw[g][:], in_=src)
            else:
                nc.vector.tensor_copy(out=xw[g][:], in_=src)

        free = list(range(8))
        holder = {}

        def take(key):
            b = free[0]
            free.remove(b)
            holder[key] = b
            return "bank%d" % b

        def give(key):
            free.append(holder[key])

        sel = {}
        pts = {}
        xg = {}
        xq = {}
        xs = {}

        def select(j):
            g, i = where[j]
            L = COPIES[g]
            sel[j] = keep.tile([P, L * P], F32, name="sel%d" % j)
            nc.vector.tensor_scalar(
                out=sel[j][:], in0=colv[:, 0 : L * P],
                scalar1=cls[g][:, i : i + 1], scalar2=None, op0=ALU.is_equal,
            )

        def transposes(j):
            g, i = where[j]
            L = COPIES[g]
            for h in range(L // 2):
                pts[(j, h)] = psum.tile([P, 2, 2, P], F32, tag=take(("t", j, h)), name="pt%d_%d" % (j, h))
                for u in range(2):
                    for c in range(2):
                        s = (2 * h + c) * P
                        if g in xw:
                            words = xw[g][:, i, u, :]
                        else:
                            words = xh[g][:, i, :].bitcast(F32)[:, u : 2 * P - 1 + u : 2]
                        nc.tensor.transpose(
                            out=pts[(j, h)][:, c, u, :], in_=words, identity=sel[j][:, s : s + P]
                        )
            xg[j] = keep.tile([P, L * P * 4], BF16, name="xg%d" % j, align_bytes=256)

        def copy_x(j):
            L = COPIES[where[j][0]]
            dst = xg[j][:].bitcast(F32).rearrange("p (l t u) -> p l t u", l=L, u=2)
            for h in range(L // 2):
                src = pts[(j, h)][:].rearrange("p l u t -> p l t u")
                if (j, h) in VECTOR_COPIES:
                    nc.vector.tensor_copy(out=dst[:, 2 * h : 2 * h + 2, :, :], in_=src)
                else:
                    nc.scalar.copy(out=dst[:, 2 * h : 2 * h + 2, :, :], in_=src)
                give(("t", j, h))

        wg = [keep.tile([P, F, 4], BF16, name="wg%d" % k, align_bytes=256) for k in range(NE)]
        wq = [keep.tile([P, F], U32, name="wq%d" % k, align_bytes=256) for k in range(NE)]
        ws = [keep.tile([P, F], U8, name="ws%d" % k, align_bytes=256) for k in range(NE)]

        def regroup_views(k, cols):
            return (
                wg[k][:, cols, :].rearrange("p (c i) t -> p c t i", i=4),
                raw[k][:, :, cols].rearrange("p t (c i) -> p c t i", i=4),
            )

        def regroup_vector(k):
            if FV[k] > 0:
                dst, src = regroup_views(k, slice(0, FV[k]))
                nc.vector.tensor_copy(out=dst, in_=src)

        def regroup_scalar(k):
            if FV[k] < F:
                dst, src = regroup_views(k, slice(FV[k], F))
                nc.scalar.copy(out=dst, in_=src)

        ready_x = []
        ready_w = []

        def quantise(item):
            what, n = item
            if what == "x":
                L = COPIES[where[n][0]]
                xq[n] = keep.tile([P, L * P], U32, name="xq%d" % n, align_bytes=256)
                xs[n] = keep.tile([P, L * P], U8, name="xs%d" % n, align_bytes=256)
                nc.vector.quantize_mx(out=xq[n][:].bitcast(FP8X4), scales=xs[n][:], in_=xg[n][:])
                ready_x.append(n)
            else:
                nc.vector.quantize_mx(
                    out=wq[n][:].bitcast(FP8X4), scales=ws[n][:],
                    in_=wg[n][:].rearrange("p f t -> p (f t)"),
                )
                ready_w.append(n)

        acc = {}
        used = {}
        part = {}
        waiting = []

        def mx(j, k, dst, cols, first, last):
            c = k % COPIES[where[j][0]]
            nc.tensor.matmul_mx(
                out=dst,
                lhsT=xq[j][:, c * P : (c + 1) * P].bitcast(FP8X4),
                lhsT_scale=xs[j][:, c * P : (c + 1) * P],
                rhs=wq[k][:, cols].bitcast(FP8X4),
                rhs_scale=ws[k][:, cols],
                start=first,
                stop=last,
            )

        def read(j, r, src, cols):
            g, i = where[j]
            R = NE // COPIES[g]
            if (j, r) not in part:
                part[(j, r)] = keep.tile([P, F], F32, name="part%d_%d" % (j, r))
            dst = part[(j, r)][:, cols]
            m = r * 3 // (R - 1)
            mask = hot[g][:, i, m : m + 1]
            if r > 0:
                nc.vector.scalar_tensor_tensor(
                    out=dst, in0=src, scalar=mask, in1=part[(j, r - 1)][:, cols],
                    op0=ALU.mult, op1=ALU.add,
                )
            elif j in VECTOR_PARTS:
                nc.vector.tensor_scalar(out=dst, in0=src, scalar1=mask, scalar2=None, op0=ALU.mult)
            else:
                nc.scalar.activation(out=dst, in_=src, func=ACT.Copy, scale=mask)
            if r == R - 1:
                nc.sync.dma_start(out=o_v[:, j, cols], in_=dst)

        def reads(n):
            for kind in (0, 1):
                for q in [q for q in waiting if min(q[2], 1) == kind]:
                    step, j, r = q
                    if n is None or step + (SUM if r > 0 else PART) <= n:
                        read(j, r, acc[(j, r)][:], slice(0, F))
                        give(("a", j, r))
                        waiting.remove(q)

        last = NT - 1

        def passes(n):
            for j in sorted(ready_x):
                L = COPIES[where[j][0]]
                R = NE // L
                for r in range(R):
                    if j == last and r == R - 1:
                        continue
                    ks = [k for k in range(r * L, r * L + L) if k in ready_w and (j, k) not in used]
                    if not ks:
                        continue
                    if (j, r) not in acc:
                        if r > 0 and (j, r - 1) not in part:
                            break
                        if len(free) <= (SPARE if len(pts) < sum(COPIES[where[q][0]] // 2 for q in range(NT)) else 0):
                            continue
                        open_last = [
                            q for q in acc
                            if q[1] == NE // COPIES[where[q[0]][0]] - 1
                            and len([k for k in range(NE) if (q[0], k) in used and k // COPIES[where[q[0]][0]] == q[1]])
                            < COPIES[where[q[0]][0]]
                        ]
                        if r == R - 1 and len(open_last) >= MAX_LAST and len(ks) < L:
                            continue
                        acc[(j, r)] = psum.tile([P, F], F32, tag=take(("a", j, r)), name="acc%d_%d" % (j, r))
                    for k in ks:
                        n_used = len([q for q in range(r * L, r * L + L) if (j, q) in used])
                        mx(j, k, acc[(j, r)][:], slice(0, F), n_used == 0, n_used == L - 1)
                        used[(j, k)] = True
                    if len([q for q in range(r * L, r * L + L) if (j, q) in used]) == L:
                        waiting.append((n, j, r))

        begun = []
        masked = []

        def at(n):
            return ITEMS[n] if 0 <= n < len(ITEMS) else None

        for n in range(-8, len(ITEMS)):
            item = at(n + FRONT)
            if item and item[0] == "x":
                select(item[1])
            item = at(n + CLASSES)
            if item and item[0] == "x" and where[item[1]][0] not in begun:
                begun.append(where[item[1]][0])
                classes(where[item[1]][0])
            if 0 <= n:
                quantise(ITEMS[n])
            item = at(n + FRONT)
            if item and item[0] == "x":
                transposes(item[1])
            item = at(n + REGROUP_V)
            if item and item[0] == "w":
                regroup_vector(item[1])
            reads(n)
            item = at(n + REGROUP_S)
            if item and item[0] == "w":
                regroup_scalar(item[1])
            item = at(n + COPY)
            if item and item[0] == "x":
                copy_x(item[1])
            item = at(n + MASKS)
            if item and item[0] == "x" and where[item[1]][0] not in masked:
                masked.append(where[item[1]][0])
                masks(where[item[1]][0])
            if n >= 0:
                passes(n)
        while waiting or len(used) < NT * NE - COPIES[where[last][0]]:
            reads(None)
            passes(len(ITEMS))
        L = COPIES[where[last][0]]
        for half in range(2):
            cols = slice(half * (F // 2), (half + 1) * (F // 2))
            ps = psum.tile([P, F // 2], F32, tag=take(("l", half)), name="last%d" % half)
            for k in range(NE - L, NE):
                mx(last, k, ps[:], cols, k == NE - L, k == NE - 1)
            read(last, NE // L - 1, ps[:], cols)
